import numpy as np
import ml_dtypes


def mxq(x, axis, fmt="e4m3"):
    dtype, down = {"e4m3": (ml_dtypes.float8_e4m3fn, 7), "e5m2": (ml_dtypes.float8_e5m2, 14)}[fmt]
    v = np.moveaxis(np.asarray(x, np.float32).astype(ml_dtypes.bfloat16).astype(np.float64), axis, -1)
    blocks = v.reshape(v.shape[:-1] + (-1, 32))
    amax = np.abs(blocks).max(-1, keepdims=True)
    byte = np.maximum(np.where(amax > 0, np.frexp(amax)[1] - 1 + 127, 0) - down, 1)
    scale = np.exp2(byte - 127.0)
    codes = (blocks / scale).astype(np.float32).astype(dtype).astype(np.float64)
    return np.moveaxis((codes * scale).reshape(v.shape), -1, axis)


WIDE = False


def mx_kscale(k):
    if not WIDE:
        return np.ones(k)
    levels = np.array([10, -10, 5, -5, 0])
    a = np.random.permutation(np.resize(levels, k // 512 * 4)).reshape(k // 512, 4)
    idx = np.arange(k)
    return np.exp2(a[idx // 512, idx % 128 // 32])


BF16 = ml_dtypes.bfloat16


def bf(x):
    return np.asarray(x, np.float32).astype(BF16)


def f64(x):
    return np.asarray(x).astype(np.float64)


N, K, F, H, O, Q, GS, SO = 1024, 8, 1024, 512, 256, 1024, 3, 2


def setup_inputs():
    s, t = mx_kscale(F), mx_kscale(H)
    return {"x": bf(np.random.standard_normal((N, F)) * s),
            "contexts": bf(np.random.standard_normal((N, K, F)) * s),
            "attn": bf(np.random.random((N, K))),
            "Wn": bf(np.random.standard_normal((H, F)) * 0.5 / np.sqrt(F) / s * t[:, None]),
            "bn": bf(np.random.standard_normal(H) * 0.1 * t),
            "Wc": bf(np.random.standard_normal((H, F)) * 1.5 / np.sqrt(F) / s * t[:, None]),
            "bc": bf(np.random.standard_normal(H) * 0.1 * t),
            "Wu": bf(np.random.standard_normal((O, H)) * 1.5 / np.sqrt(H) / t),
            "bu": bf(np.random.standard_normal(O) * 0.1)}


def reference(x, contexts, attn, Wn, bn, Wc, bc, Wu, bu):
    xt = (mxq(f64(x), 1, "e4m3") @ mxq(f64(Wn).T, 0, "e4m3")) + f64(bn)
    ct = (mxq(f64(contexts).reshape(N * K, F), 1, "e4m3") @ mxq(f64(Wc).T, 0, "e4m3")).reshape(N, K, H) + f64(bc)
    ca = (ct * f64(attn)[..., None]).mean(axis=1)
    return (mxq(xt + ca, 1, "e4m3") @ mxq(f64(Wu).T, 0, "e4m3")) + f64(bu)

@@ -1,0 +1,263 @@
+from contextlib import ExitStack
+
+import concourse.mybir as mybir
+from concourse.masks import make_identity
+
+F32 = mybir.dt.float32
+BF16 = mybir.dt.bfloat16
+U32 = mybir.dt.uint32
+U8 = mybir.dt.uint8
+FP8X4 = mybir.dt.float8_e4m3fn_x4
+ALU = mybir.AluOpType
+
+P = 128
+PACK = 4
+K_PASS = P * PACK
+
+NODES, CONTEXTS, FEATURES, HIDDEN, OUTPUTS = 1024, 8, 1024, 512, 256
+NODE_TILES = NODES // P
+PASSES = FEATURES // K_PASS
+WORD_COLUMNS = FEATURES // 2 // P
+
+BLOCKS = 4
+X_ROUNDS = NODE_TILES // BLOCKS
+ROUNDS = X_ROUNDS + NODE_TILES * CONTEXTS // BLOCKS
+ONE = CONTEXTS
+
+RAW_BUFS = 10
+BLOCK_BUFS = 3 * BLOCKS
+
+FLOPS = 2 * NODES * (CONTEXTS + 1) * FEATURES * HIDDEN + 2 * NODES * HIDDEN * OUTPUTS
+
+
+def tile_nodeembeddinglayer_pa_t_kernel(tc, x, contexts, attn, Wn, bn, Wc, bc, Wu, bu, out):
+    nc = tc.nc
+    with ExitStack() as stack:
+        keep = stack.enter_context(tc.tile_pool(name="keep", bufs=1))
+        raw_pool = stack.enter_context(tc.tile_pool(name="raw_pool", bufs=RAW_BUFS))
+        block_pool = stack.enter_context(tc.tile_pool(name="block_pool", bufs=BLOCK_BUFS))
+        tail_pool = stack.enter_context(tc.tile_pool(name="tail_pool", bufs=2))
+        flip_banks = stack.enter_context(tc.psum_pool(name="flip_banks", bufs=BLOCKS))
+        sum_banks = stack.enter_context(tc.psum_pool(name="sum_banks", bufs=BLOCKS))
+
+        x_blocks = x.rearrange("(p t) f -> p t f", t=NODE_TILES)
+        context_blocks = contexts.rearrange("(p t) k f -> p (t k) f", t=NODE_TILES)
+        out_tiles = out.rearrange("(p t) o -> p t o", t=NODE_TILES)
+
+        def load_weights(w, label):
+            raw = keep.tile([P, HIDDEN // P, FEATURES], BF16, name=label + "_raw")
+            nc.sync.dma_start(out=raw[:], in_=w.rearrange("(b p) f -> p b f", p=P))
+            return raw
+
+        def load_round(r):
+            raw = raw_pool.tile([P, BLOCKS, FEATURES], BF16)
+            if r < X_ROUNDS:
+                rows = x_blocks[:, r * BLOCKS : (r + 1) * BLOCKS, :]
+            else:
+                rows = context_blocks[:, (r - X_ROUNDS) * BLOCKS : (r - X_ROUNDS + 1) * BLOCKS, :]
+            nc.sync.dma_start(out=raw[:], in_=rows)
+            return raw
+
+        attn_sb = keep.tile([P, NODE_TILES, CONTEXTS], BF16)
+        nc.scalar.dma_start(out=attn_sb[:], in_=attn.rearrange("(p t) k -> p t k", t=NODE_TILES))
+        BN, BC, BU = slice(0, HIDDEN), slice(HIDDEN, 2 * HIDDEN), slice(2 * HIDDEN, 2 * HIDDEN + OUTPUTS)
+        bias_rows = keep.tile([P, 2 * HIDDEN + OUTPUTS], BF16)
+        nc.vector.memset(bias_rows[:], 0.0)
+        nc.scalar.dma_start(out=bias_rows[0:1, BN], in_=bn.unsqueeze(0))
+        nc.scalar.dma_start(out=bias_rows[0:1, BC], in_=bc.unsqueeze(0))
+        nc.scalar.dma_start(out=bias_rows[0:1, BU], in_=bu.unsqueeze(0))
+
+        wn_raw = load_weights(Wn, "wn")
+        raws = {}
+        for r in range(X_ROUNDS):
+            raws[r] = load_round(r)
+        wc_raw = load_weights(Wc, "wc")
+        wu_raw = keep.tile([P, OUTPUTS // P, HIDDEN], BF16)
+        nc.sync.dma_start(out=wu_raw[:], in_=Wu.rearrange("(b p) h -> p b h", p=P))
+        for r in range(X_ROUNDS, RAW_BUFS):
+            raws[r] = load_round(r)
+
+        identity_f32 = keep.tile([P, P], F32)
+        make_identity(nc, identity_f32[:])
+        identity_bf16 = keep.tile([P, P], BF16)
+        make_identity(nc, identity_bf16[:])
+        ones = keep.tile([P, P], BF16)
+        nc.vector.memset(ones[:], 1.0)
+
+        bias_all = keep.tile([P, 2 * HIDDEN + OUTPUTS], F32)
+        for cols, width in ((BN, HIDDEN), (BC, HIDDEN), (BU, OUTPUTS)):
+            spread = sum_banks.tile([P, width], F32, tag="sums")
+            nc.tensor.matmul(out=spread[:], lhsT=ones[:], rhs=bias_rows[:, cols], start=True, stop=True)
+            nc.scalar.copy(out=bias_all[:, cols], in_=spread[:])
+
+        weight = keep.tile([P, NODE_TILES, CONTEXTS + 1], F32)
+        nc.vector.memset(weight[:], 1.0)
+        nc.vector.tensor_scalar_mul(out=weight[:, :, 0:CONTEXTS], in0=attn_sb[:], scalar1=1.0 / CONTEXTS)
+        weight_sum = keep.tile([P, NODE_TILES], F32)
+        nc.vector.tensor_reduce(
+            out=weight_sum[:], in_=weight[:, :, 0:CONTEXTS], axis=mybir.AxisListType.X, op=ALU.add
+        )
+        running = keep.tile([P, NODE_TILES, HIDDEN], F32)
+        for t in range(NODE_TILES):
+            nc.vector.scalar_tensor_tensor(
+                out=running[:, t, :],
+                in0=bias_all[:, BC],
+                scalar=weight_sum[:, t : t + 1],
+                in1=bias_all[:, BN],
+                op0=ALU.mult,
+                op1=ALU.add,
+            )
+
+        def flip_block(words, grouped_words):
+            flipped = flip_banks.tile([P, WORD_COLUMNS, P], F32, tag="flipped")
+            for c in range(WORD_COLUMNS):
+                nc.tensor.transpose(flipped[:, c, :], words[:, c * P : (c + 1) * P], identity_f32[:])
+            nc.scalar.copy(out=grouped_words, in_=flipped[:].rearrange("p (g u) r -> p g r u", u=2))
+
+        def flip_round(r):
+            words = raws[r][:].bitcast(F32)
+            grouped_blocks = []
+            for j in range(BLOCKS):
+                grouped = block_pool.tile([P, PASSES * P * PACK], BF16, align_bytes=64)
+                flip_block(
+                    words[:, j, :],
+                    grouped[:].bitcast(F32).rearrange("p (g r u) -> p g r u", g=PASSES, u=2),
+                )
+                grouped_blocks.append(grouped)
+            if r + RAW_BUFS < ROUNDS:
+                raws[r + RAW_BUFS] = load_round(r + RAW_BUFS)
+            return grouped_blocks
+
+        def quantise_block(grouped):
+            codes = block_pool.tile([P, PASSES * P], U32, align_bytes=64)
+            scales = block_pool.tile([P, PASSES * P], U8, align_bytes=64)
+            nc.vector.quantize_mx(out=codes[:].bitcast(FP8X4), scales=scales[:], in_=grouped[:])
+            return codes, scales
+
+        def prepare_weights(raw, label):
+            words = raw[:].bitcast(F32)
+            grouped = keep.tile([P, PASSES * HIDDEN * PACK], BF16, align_bytes=64, name=label + "_grouped")
+            by_block = grouped[:].bitcast(F32).rearrange("p (g b r u) -> p b g r u", g=PASSES, b=HIDDEN // P, u=2)
+            for b in range(HIDDEN // P):
+                flip_block(words[:, b, :], by_block[:, b])
+            codes = keep.tile([P, PASSES * HIDDEN], U32, align_bytes=64, name=label + "_codes")
+            scales = keep.tile([P, PASSES * HIDDEN], U8, align_bytes=64, name=label + "_scales")
+            nc.vector.quantize_mx(out=codes[:].bitcast(FP8X4), scales=scales[:], in_=grouped[:])
+            return codes, scales
+
+        def multiply_block(operand, weights):
+            codes, scales = operand
+            w_codes, w_scales = weights
+            sums = sum_banks.tile([P, HIDDEN], F32, tag="sums")
+            for g in range(PASSES):
+                rows = slice(g * P, (g + 1) * P)
+                hidden_cols = slice(g * HIDDEN, (g + 1) * HIDDEN)
+                nc.tensor.matmul_mx(
+                    out=sums[:],
+                    lhsT=codes[:, rows].bitcast(FP8X4),
+                    lhsT_scale=scales[:, rows],
+                    rhs=w_codes[:, hidden_cols].bitcast(FP8X4),
+                    rhs_scale=w_scales[:, hidden_cols],
+                    start=(g == 0),
+                    stop=(g == PASSES - 1),
+                )
+            return sums
+
+        def add_weighted(sums, t, column, target):
+            nc.vector.scalar_tensor_tensor(
+                out=target,
+                in0=sums[:],
+                scalar=weight[:, t, column : column + 1],
+                in1=running[:, t, :],
+                op0=ALU.mult,
+                op1=ALU.add,
+            )
+
+        def flip_hidden(rows, grouped):
+            flipped = flip_banks.tile([P, PACK, P], BF16, tag="flipped")
+            for c in range(PACK):
+                nc.tensor.transpose(flipped[:, c, :], rows[:, c * P : (c + 1) * P], identity_bf16[:])
+            nc.scalar.copy(out=grouped, in_=flipped[:].rearrange("p c r -> p r c"))
+
+        def prepare_wu():
+            grouped = keep.tile([P, OUTPUTS, PACK], BF16, align_bytes=64, name="wu_grouped")
+            for b in range(OUTPUTS // P):
+                flip_hidden(wu_raw[:, b, :], grouped[:, b * P : (b + 1) * P, :])
+            codes = keep.tile([P, OUTPUTS], U32, align_bytes=64, name="wu_codes")
+            scales = keep.tile([P, OUTPUTS], U8, align_bytes=64, name="wu_scales")
+            nc.vector.quantize_mx(
+                out=codes[:].bitcast(FP8X4), scales=scales[:], in_=grouped[:].rearrange("p o c -> p (o c)")
+            )
+            return codes, scales
+
+        def quantise_hidden(grouped):
+            codes = tail_pool.tile([P, P], U32, align_bytes=64, name="hidden_codes")
+            scales = tail_pool.tile([P, P], U8, align_bytes=64, name="hidden_scales")
+            nc.vector.quantize_mx(
+                out=codes[:].bitcast(FP8X4), scales=scales[:], in_=grouped[:].rearrange("p r c -> p (r c)")
+            )
+            return codes, scales
+
+        def project(operand, weights, t):
+            codes, scales = operand
+            w_codes, w_scales = weights
+            projected = sum_banks.tile([P, OUTPUTS], F32, tag="sums")
+            nc.tensor.matmul_mx(
+                out=projected[:],
+                lhsT=codes[:].bitcast(FP8X4),
+                lhsT_scale=scales[:],
+                rhs=w_codes[:].bitcast(FP8X4),
+                rhs_scale=w_scales[:],
+                start=True,
+                stop=True,
+            )
+            result = tail_pool.tile([P, OUTPUTS], F32)
+            nc.vector.tensor_tensor(out=result[:], in0=projected[:], in1=bias_all[:, BU], op=ALU.add)
+            nc.sync.dma_start(out=out_tiles[:, t, :], in_=result[:])
+
+        def tile_finished_in(r):
+            contexts_done = (r + 1 - X_ROUNDS) * BLOCKS
+            if X_ROUNDS <= r < ROUNDS and contexts_done % CONTEXTS == 0:
+                return contexts_done // CONTEXTS - 1
+            return None
+
+        wn = prepare_weights(wn_raw, "wn")
+        wc = None
+        wu = None
+        operands = [quantise_block(grouped) for grouped in flip_round(0)]
+        hidden_of = {}
+        hidden_operand_of = {}
+        for r in range(ROUNDS + 2):
+            if r + 1 == X_ROUNDS:
+                wc = prepare_weights(wc_raw, "wc")
+                wu = prepare_wu()
+            grouped_blocks = []
+            if r + 1 < ROUNDS:
+                grouped_blocks = flip_round(r + 1)
+            flipping = tile_finished_in(r - 1)
+            if flipping is not None:
+                hidden_grouped = tail_pool.tile([P, P, PACK], BF16, align_bytes=64)
+                flip_hidden(hidden_of[flipping][:], hidden_grouped[:])
+
+            following = []
+            for j in range(BLOCKS):
+                if r + 1 < ROUNDS:
+                    following.append(quantise_block(grouped_blocks[j]))
+                if r < X_ROUNDS:
+                    t = r * BLOCKS + j
+                    add_weighted(multiply_block(operands[j], wn), t, ONE, running[:, t, :])
+                elif r < ROUNDS:
+                    t, k = divmod((r - X_ROUNDS) * BLOCKS + j, CONTEXTS)
+                    if k < CONTEXTS - 1:
+                        add_weighted(multiply_block(operands[j], wc), t, k, running[:, t, :])
+                    else:
+                        hidden = tail_pool.tile([P, HIDDEN], BF16)
+                        add_weighted(multiply_block(operands[j], wc), t, k, hidden[:])
+                        hidden_of[t] = hidden
+            operands = following
+
+            projecting = tile_finished_in(r - 2)
+            if projecting is not None:
+                project(hidden_operand_of[projecting], wu, projecting)
+            if flipping is not None:
+                hidden_operand_of[flipping] = quantise_hidden(hidden_grouped)

@@ -17,14 +17,17 @@ K_PASS = P * PACK
 NODES, CONTEXTS, FEATURES, HIDDEN, OUTPUTS = 1024, 8, 1024, 512, 256
 NODE_TILES = NODES // P
 PASSES = FEATURES // K_PASS
-WORD_COLUMNS = FEATURES // 2 // P
+WORD_PIECES = FEATURES // 2 // P
 
 BLOCKS = 4
-X_ROUNDS = NODE_TILES // BLOCKS
-ROUNDS = X_ROUNDS + NODE_TILES * CONTEXTS // BLOCKS
+WN_ROUND = 0
+X_ROUND = 1
+WC_ROUND = X_ROUND + NODE_TILES // BLOCKS
+CONTEXT_ROUND = WC_ROUND + 1
+ROUNDS = CONTEXT_ROUND + NODE_TILES * CONTEXTS // BLOCKS
 ONE = CONTEXTS
 
-RAW_BUFS = 10
+RAW_BUFS = 10 * BLOCKS
 BLOCK_BUFS = 3 * BLOCKS
 
 FLOPS = 2 * NODES * (CONTEXTS + 1) * FEATURES * HIDDEN + 2 * NODES * HIDDEN * OUTPUTS
@@ -39,43 +42,42 @@ def tile_nodeembeddinglayer_pa_t_kernel(tc, x, contexts, attn, Wn, bn, Wc, bc, W
         tail_pool = stack.enter_context(tc.tile_pool(name="tail_pool", bufs=2))
         flip_banks = stack.enter_context(tc.psum_pool(name="flip_banks", bufs=BLOCKS))
         sum_banks = stack.enter_context(tc.psum_pool(name="sum_banks", bufs=BLOCKS))
-
-        x_blocks = x.rearrange("(p t) f -> p t f", t=NODE_TILES)
-        context_blocks = contexts.rearrange("(p t) k f -> p (t k) f", t=NODE_TILES)
-        out_tiles = out.rearrange("(p t) o -> p t o", t=NODE_TILES)
-
-        def load_weights(w, label):
-            raw = keep.tile([P, HIDDEN // P, FEATURES], BF16, name=label + "_raw")
-            nc.sync.dma_start(out=raw[:], in_=w.rearrange("(b p) f -> p b f", p=P))
-            return raw
-
-        def load_round(r):
-            raw = raw_pool.tile([P, BLOCKS, FEATURES], BF16)
-            if r < X_ROUNDS:
-                rows = x_blocks[:, r * BLOCKS : (r + 1) * BLOCKS, :]
-            else:
-                rows = context_blocks[:, (r - X_ROUNDS) * BLOCKS : (r - X_ROUNDS + 1) * BLOCKS, :]
-            nc.sync.dma_start(out=raw[:], in_=rows)
-            return raw
+        stack.enter_context(tc.manual_schedule())
 
         attn_sb = keep.tile([P, NODE_TILES, CONTEXTS], BF16)
-        nc.scalar.dma_start(out=attn_sb[:], in_=attn.rearrange("(p t) k -> p t k", t=NODE_TILES))
-        BN, BC, BU = slice(0, HIDDEN), slice(HIDDEN, 2 * HIDDEN), slice(2 * HIDDEN, 2 * HIDDEN + OUTPUTS)
+        nc.sync.dma_start(out=attn_sb[:], in_=attn.rearrange("(p t) k -> p t k", t=NODE_TILES))
+        BC, BN, BU = slice(0, HIDDEN), slice(HIDDEN, 2 * HIDDEN), slice(2 * HIDDEN, 2 * HIDDEN + OUTPUTS)
         bias_rows = keep.tile([P, 2 * HIDDEN + OUTPUTS], BF16)
         nc.vector.memset(bias_rows[:], 0.0)
-        nc.scalar.dma_start(out=bias_rows[0:1, BN], in_=bn.unsqueeze(0))
-        nc.scalar.dma_start(out=bias_rows[0:1, BC], in_=bc.unsqueeze(0))
-        nc.scalar.dma_start(out=bias_rows[0:1, BU], in_=bu.unsqueeze(0))
+        nc.sync.dma_start(out=bias_rows[0:1, BC], in_=bc.unsqueeze(0))
+        nc.sync.dma_start(out=bias_rows[0:1, BN], in_=bn.unsqueeze(0))
+        nc.sync.dma_start(out=bias_rows[0:1, BU], in_=bu.unsqueeze(0))
 
-        wn_raw = load_weights(Wn, "wn")
-        raws = {}
-        for r in range(X_ROUNDS):
-            raws[r] = load_round(r)
-        wc_raw = load_weights(Wc, "wc")
+        x_blocks = x.rearrange("(p t) f -> t p f", t=NODE_TILES)
+        context_blocks = contexts.rearrange("(p t) k f -> (t k) p f", t=NODE_TILES)
+        wn_blocks = Wn.rearrange("(b p) f -> b p f", p=P)
+        wc_blocks = Wc.rearrange("(b p) f -> b p f", p=P)
+        sources = (
+            [wn_blocks[b] for b in range(BLOCKS)]
+            + [x_blocks[t] for t in range(NODE_TILES)]
+            + [wc_blocks[b] for b in range(BLOCKS)]
+            + [context_blocks[c] for c in range(NODE_TILES * CONTEXTS)]
+        )
+        out_tiles = out.rearrange("(p t) o -> t p o", t=NODE_TILES)
+
+        rows_of = {}
+
+        def load_block(i):
+            raw = raw_pool.tile([P, FEATURES], BF16)
+            nc.sync.dma_start(out=raw[:], in_=sources[i])
+            rows_of[i] = raw
+
+        for i in range(CONTEXT_ROUND * BLOCKS):
+            load_block(i)
         wu_raw = keep.tile([P, OUTPUTS // P, HIDDEN], BF16)
         nc.sync.dma_start(out=wu_raw[:], in_=Wu.rearrange("(b p) h -> p b h", p=P))
-        for r in range(X_ROUNDS, RAW_BUFS):
-            raws[r] = load_round(r)
+        for i in range(CONTEXT_ROUND * BLOCKS, RAW_BUFS):
+            load_block(i)
 
         identity_f32 = keep.tile([P, P], F32)
         make_identity(nc, identity_f32[:])
@@ -85,7 +87,7 @@ def tile_nodeembeddinglayer_pa_t_kernel(tc, x, contexts, attn, Wn, bn, Wc, bc, W
         nc.vector.memset(ones[:], 1.0)
 
         bias_all = keep.tile([P, 2 * HIDDEN + OUTPUTS], F32)
-        for cols, width in ((BN, HIDDEN), (BC, HIDDEN), (BU, OUTPUTS)):
+        for cols, width in ((BC, HIDDEN), (BN, HIDDEN), (BU, OUTPUTS)):
             spread = sum_banks.tile([P, width], F32, tag="sums")
             nc.tensor.matmul(out=spread[:], lhsT=ones[:], rhs=bias_rows[:, cols], start=True, stop=True)
             nc.scalar.copy(out=bias_all[:, cols], in_=spread[:])
@@ -108,24 +110,24 @@ def tile_nodeembeddinglayer_pa_t_kernel(tc, x, contexts, attn, Wn, bn, Wc, bc, W
                 op1=ALU.add,
             )
 
-        def flip_block(words, grouped_words):
-            flipped = flip_banks.tile([P, WORD_COLUMNS, P], F32, tag="flipped")
-            for c in range(WORD_COLUMNS):
+        def flip_block(i, grouped_words):
+            words = rows_of[i][:].bitcast(F32)
+            flipped = flip_banks.tile([P, WORD_PIECES, P], F32, tag="flipped")
+            for c in range(WORD_PIECES):
                 nc.tensor.transpose(flipped[:, c, :], words[:, c * P : (c + 1) * P], identity_f32[:])
             nc.scalar.copy(out=grouped_words, in_=flipped[:].rearrange("p (g u) r -> p g r u", u=2))
+            if i + RAW_BUFS < len(sources):
+                load_block(i + RAW_BUFS)
 
-        def flip_round(r):
-            words = raws[r][:].bitcast(F32)
+        def flip_round(q):
             grouped_blocks = []
             for j in range(BLOCKS):
                 grouped = block_pool.tile([P, PASSES * P * PACK], BF16, align_bytes=64)
                 flip_block(
-                    words[:, j, :],
+                    q * BLOCKS + j,
                     grouped[:].bitcast(F32).rearrange("p (g r u) -> p g r u", g=PASSES, u=2),
                 )
                 grouped_blocks.append(grouped)
-            if r + RAW_BUFS < ROUNDS:
-                raws[r + RAW_BUFS] = load_round(r + RAW_BUFS)
             return grouped_blocks
 
         def quantise_block(grouped):
@@ -134,12 +136,14 @@ def tile_nodeembeddinglayer_pa_t_kernel(tc, x, contexts, attn, Wn, bn, Wc, bc, W
             nc.vector.quantize_mx(out=codes[:].bitcast(FP8X4), scales=scales[:], in_=grouped[:])
             return codes, scales
 
-        def prepare_weights(raw, label):
-            words = raw[:].bitcast(F32)
+        def flip_weights(q, label):
             grouped = keep.tile([P, PASSES * HIDDEN * PACK], BF16, align_bytes=64, name=label + "_grouped")
-            by_block = grouped[:].bitcast(F32).rearrange("p (g b r u) -> p b g r u", g=PASSES, b=HIDDEN // P, u=2)
-            for b in range(HIDDEN // P):
-                flip_block(words[:, b, :], by_block[:, b])
+            by_block = grouped[:].bitcast(F32).rearrange("p (g b r u) -> p b g r u", g=PASSES, b=BLOCKS, u=2)
+            for b in range(BLOCKS):
+                flip_block(q * BLOCKS + b, by_block[:, b])
+            return grouped
+
+        def quantise_weights(grouped, label):
             codes = keep.tile([P, PASSES * HIDDEN], U32, align_bytes=64, name=label + "_codes")
             scales = keep.tile([P, PASSES * HIDDEN], U8, align_bytes=64, name=label + "_scales")
             nc.vector.quantize_mx(out=codes[:].bitcast(FP8X4), scales=scales[:], in_=grouped[:])
@@ -179,20 +183,9 @@ def tile_nodeembeddinglayer_pa_t_kernel(tc, x, contexts, attn, Wn, bn, Wc, bc, W
                 nc.tensor.transpose(flipped[:, c, :], rows[:, c * P : (c + 1) * P], identity_bf16[:])
             nc.scalar.copy(out=grouped, in_=flipped[:].rearrange("p c r -> p r c"))
 
-        def prepare_wu():
-            grouped = keep.tile([P, OUTPUTS, PACK], BF16, align_bytes=64, name="wu_grouped")
-            for b in range(OUTPUTS // P):
-                flip_hidden(wu_raw[:, b, :], grouped[:, b * P : (b + 1) * P, :])
-            codes = keep.tile([P, OUTPUTS], U32, align_bytes=64, name="wu_codes")
-            scales = keep.tile([P, OUTPUTS], U8, align_bytes=64, name="wu_scales")
-            nc.vector.quantize_mx(
-                out=codes[:].bitcast(FP8X4), scales=scales[:], in_=grouped[:].rearrange("p o c -> p (o c)")
-            )
-            return codes, scales
-
-        def quantise_hidden(grouped):
-            codes = tail_pool.tile([P, P], U32, align_bytes=64, name="hidden_codes")
-            scales = tail_pool.tile([P, P], U8, align_bytes=64, name="hidden_scales")
+        def quantise_hidden(grouped, pool, label, count):
+            codes = pool.tile([P, count], U32, align_bytes=64, name=label + "_codes")
+            scales = pool.tile([P, count], U8, align_bytes=64, name=label + "_scales")
             nc.vector.quantize_mx(
                 out=codes[:].bitcast(FP8X4), scales=scales[:], in_=grouped[:].rearrange("p r c -> p (r c)")
             )
@@ -213,51 +206,60 @@ def tile_nodeembeddinglayer_pa_t_kernel(tc, x, contexts, attn, Wn, bn, Wc, bc, W
             )
             result = tail_pool.tile([P, OUTPUTS], F32)
             nc.vector.tensor_tensor(out=result[:], in0=projected[:], in1=bias_all[:, BU], op=ALU.add)
-            nc.sync.dma_start(out=out_tiles[:, t, :], in_=result[:])
+            nc.sync.dma_start(out=out_tiles[t], in_=result[:])
 
-        def tile_finished_in(r):
-            contexts_done = (r + 1 - X_ROUNDS) * BLOCKS
-            if X_ROUNDS <= r < ROUNDS and contexts_done % CONTEXTS == 0:
+        def tile_finished_in(q):
+            contexts_done = (q + 1 - CONTEXT_ROUND) * BLOCKS
+            if CONTEXT_ROUND <= q < ROUNDS and contexts_done % CONTEXTS == 0:
                 return contexts_done // CONTEXTS - 1
             return None
 
-        wn = prepare_weights(wn_raw, "wn")
-        wc = None
-        wu = None
-        operands = [quantise_block(grouped) for grouped in flip_round(0)]
+        weights_of = {}
         hidden_of = {}
-        hidden_operand_of = {}
-        for r in range(ROUNDS + 2):
-            if r + 1 == X_ROUNDS:
-                wc = prepare_weights(wc_raw, "wc")
-                wu = prepare_wu()
-            grouped_blocks = []
-            if r + 1 < ROUNDS:
-                grouped_blocks = flip_round(r + 1)
-            flipping = tile_finished_in(r - 1)
-            if flipping is not None:
-                hidden_grouped = tail_pool.tile([P, P, PACK], BF16, align_bytes=64)
-                flip_hidden(hidden_of[flipping][:], hidden_grouped[:])
+        operands = []
+        for q in range(-1, ROUNDS + 2):
+            coming = q + 1
+            coming_is_weights = coming == WN_ROUND or coming == WC_ROUND
+            coming_is_rows = coming < ROUNDS and not coming_is_weights
 
+            done = tile_finished_in(q - 2)
+            if done is not None:
+                hidden_grouped = tail_pool.tile([P, P, PACK], BF16, align_bytes=64)
+                flip_hidden(hidden_of[done][:], hidden_grouped[:])
+            if coming == WN_ROUND:
+                weights_grouped = flip_weights(coming, "wn")
+            if coming == WC_ROUND:
+                weights_grouped = flip_weights(coming, "wc")
+                wu_grouped = keep.tile([P, OUTPUTS, PACK], BF16, align_bytes=64)
+                for b in range(OUTPUTS // P):
+                    flip_hidden(wu_raw[:, b, :], wu_grouped[:, b * P : (b + 1) * P, :])
+            if coming_is_rows:
+                grouped_blocks = flip_round(coming)
+
+            if done is not None:
+                hidden_operand = quantise_hidden(hidden_grouped, tail_pool, "hidden", P)
             following = []
             for j in range(BLOCKS):
-                if r + 1 < ROUNDS:
+                if coming_is_rows:
                     following.append(quantise_block(grouped_blocks[j]))
-                if r < X_ROUNDS:
-                    t = r * BLOCKS + j
-                    add_weighted(multiply_block(operands[j], wn), t, ONE, running[:, t, :])
-                elif r < ROUNDS:
-                    t, k = divmod((r - X_ROUNDS) * BLOCKS + j, CONTEXTS)
+                if X_ROUND <= q < WC_ROUND:
+                    t = (q - X_ROUND) * BLOCKS + j
+                    add_weighted(multiply_block(operands[j], weights_of["wn"]), t, ONE, running[:, t, :])
+                if CONTEXT_ROUND <= q < ROUNDS:
+                    t, k = divmod((q - CONTEXT_ROUND) * BLOCKS + j, CONTEXTS)
+                    sums = multiply_block(operands[j], weights_of["wc"])
                     if k < CONTEXTS - 1:
-                        add_weighted(multiply_block(operands[j], wc), t, k, running[:, t, :])
+                        add_weighted(sums, t, k, running[:, t, :])
                     else:
                         hidden = tail_pool.tile([P, HIDDEN], BF16)
-                        add_weighted(multiply_block(operands[j], wc), t, k, hidden[:])
+                        add_weighted(sums, t, k, hidden[:])
                         hidden_of[t] = hidden
-            operands = following
-
-            projecting = tile_finished_in(r - 2)
-            if projecting is not None:
-                project(hidden_operand_of[projecting], wu, projecting)
-            if flipping is not None:
-                hidden_operand_of[flipping] = quantise_hidden(hidden_grouped)
+            if coming_is_rows:
+                operands = following
+            if coming == WN_ROUND:
+                weights_of["wn"] = quantise_weights(weights_grouped, "wn")
+            if coming == WC_ROUND:
+                weights_of["wc"] = quantise_weights(weights_grouped, "wc")
+                weights_of["wu"] = quantise_hidden(wu_grouped, keep, "wu", OUTPUTS)
+            if done is not None:
+                project(hidden_operand, weights_of["wu"], done)

@@ -27,7 +27,7 @@ CONTEXT_ROUND = WC_ROUND + 1
 ROUNDS = CONTEXT_ROUND + NODE_TILES * CONTEXTS // BLOCKS
 ONE = CONTEXTS
 
-RAW_BUFS = 10 * BLOCKS
+RAW_BUFS = 10
 BLOCK_BUFS = 3 * BLOCKS
 
 FLOPS = 2 * NODES * (CONTEXTS + 1) * FEATURES * HIDDEN + 2 * NODES * HIDDEN * OUTPUTS
@@ -53,31 +53,29 @@ def tile_nodeembeddinglayer_pa_t_kernel(tc, x, contexts, attn, Wn, bn, Wc, bc, W
         nc.sync.dma_start(out=bias_rows[0:1, BN], in_=bn.unsqueeze(0))
         nc.sync.dma_start(out=bias_rows[0:1, BU], in_=bu.unsqueeze(0))
 
-        x_blocks = x.rearrange("(p t) f -> t p f", t=NODE_TILES)
-        context_blocks = contexts.rearrange("(p t) k f -> (t k) p f", t=NODE_TILES)
-        wn_blocks = Wn.rearrange("(b p) f -> b p f", p=P)
-        wc_blocks = Wc.rearrange("(b p) f -> b p f", p=P)
+        x_blocks = x.rearrange("(p t) f -> p t f", t=NODE_TILES)
+        context_blocks = contexts.rearrange("(p t) k f -> p (t k) f", t=NODE_TILES)
         sources = (
-            [wn_blocks[b] for b in range(BLOCKS)]
-            + [x_blocks[t] for t in range(NODE_TILES)]
-            + [wc_blocks[b] for b in range(BLOCKS)]
-            + [context_blocks[c] for c in range(NODE_TILES * CONTEXTS)]
+            [Wn.rearrange("(b p) f -> p b f", p=P)]
+            + [x_blocks[:, b : b + BLOCKS, :] for b in range(0, NODE_TILES, BLOCKS)]
+            + [Wc.rearrange("(b p) f -> p b f", p=P)]
+            + [context_blocks[:, b : b + BLOCKS, :] for b in range(0, NODE_TILES * CONTEXTS, BLOCKS)]
         )
         out_tiles = out.rearrange("(p t) o -> t p o", t=NODE_TILES)
 
         rows_of = {}
 
-        def load_block(i):
-            raw = raw_pool.tile([P, FEATURES], BF16)
-            nc.sync.dma_start(out=raw[:], in_=sources[i])
-            rows_of[i] = raw
+        def load_round(q):
+            raw = raw_pool.tile([P, BLOCKS, FEATURES], BF16)
+            nc.sync.dma_start(out=raw[:], in_=sources[q])
+            rows_of[q] = raw
 
-        for i in range(CONTEXT_ROUND * BLOCKS):
-            load_block(i)
+        for q in range(CONTEXT_ROUND):
+            load_round(q)
         wu_raw = keep.tile([P, OUTPUTS // P, HIDDEN], BF16)
         nc.sync.dma_start(out=wu_raw[:], in_=Wu.rearrange("(b p) h -> p b h", p=P))
-        for i in range(CONTEXT_ROUND * BLOCKS, RAW_BUFS):
-            load_block(i)
+        for q in range(CONTEXT_ROUND, RAW_BUFS):
+            load_round(q)
 
         identity_f32 = keep.tile([P, P], F32)
         make_identity(nc, identity_f32[:])
@@ -110,21 +108,22 @@ def tile_nodeembeddinglayer_pa_t_kernel(tc, x, contexts, attn, Wn, bn, Wc, bc, W
                 op1=ALU.add,
             )
 
-        def flip_block(i, grouped_words):
-            words = rows_of[i][:].bitcast(F32)
+        def flip_block(q, j, grouped_words):
+            words = rows_of[q][:].bitcast(F32)[:, j, :]
             flipped = flip_banks.tile([P, WORD_PIECES, P], F32, tag="flipped")
             for c in range(WORD_PIECES):
                 nc.tensor.transpose(flipped[:, c, :], words[:, c * P : (c + 1) * P], identity_f32[:])
             nc.scalar.copy(out=grouped_words, in_=flipped[:].rearrange("p (g u) r -> p g r u", u=2))
-            if i + RAW_BUFS < len(sources):
-                load_block(i + RAW_BUFS)
+            if j == BLOCKS - 1 and q + RAW_BUFS < ROUNDS:
+                load_round(q + RAW_BUFS)
 
         def flip_round(q):
             grouped_blocks = []
             for j in range(BLOCKS):
                 grouped = block_pool.tile([P, PASSES * P * PACK], BF16, align_bytes=64)
                 flip_block(
-                    q * BLOCKS + j,
+                    q,
+                    j,
                     grouped[:].bitcast(F32).rearrange("p (g r u) -> p g r u", g=PASSES, u=2),
                 )
                 grouped_blocks.append(grouped)
@@ -140,7 +139,7 @@ def tile_nodeembeddinglayer_pa_t_kernel(tc, x, contexts, attn, Wn, bn, Wc, bc, W
             grouped = keep.tile([P, PASSES * HIDDEN * PACK], BF16, align_bytes=64, name=label + "_grouped")
             by_block = grouped[:].bitcast(F32).rearrange("p (g b r u) -> p b g r u", g=PASSES, b=BLOCKS, u=2)
             for b in range(BLOCKS):
-                flip_block(q * BLOCKS + b, by_block[:, b])
+                flip_block(q, b, by_block[:, b])
             return grouped
 
         def quantise_weights(grouped, label):

from contextlib import ExitStack

import concourse.mybir as mybir
from concourse.masks import make_identity

F32 = mybir.dt.float32
BF16 = mybir.dt.bfloat16
U32 = mybir.dt.uint32
U8 = mybir.dt.uint8
FP8X4 = mybir.dt.float8_e4m3fn_x4
ALU = mybir.AluOpType

P = 128
PACK = 4
K_PASS = P * PACK

NODES, CONTEXTS, FEATURES, HIDDEN, OUTPUTS = 1024, 8, 1024, 512, 256
NODE_TILES = NODES // P
PASSES = FEATURES // K_PASS
WORD_PIECES = FEATURES // 2 // P

BLOCKS = 4
WN_ROUND = 0
X_ROUND = 1
WC_ROUND = X_ROUND + NODE_TILES // BLOCKS
CONTEXT_ROUND = WC_ROUND + 1
ROUNDS = CONTEXT_ROUND + NODE_TILES * CONTEXTS // BLOCKS
ONE = CONTEXTS

RAW_BUFS = 10
BLOCK_BUFS = 3 * BLOCKS

FLOPS = 2 * NODES * (CONTEXTS + 1) * FEATURES * HIDDEN + 2 * NODES * HIDDEN * OUTPUTS


def tile_nodeembeddinglayer_pa_t_kernel(tc, x, contexts, attn, Wn, bn, Wc, bc, Wu, bu, out):
    nc = tc.nc
    with ExitStack() as stack:
        keep = stack.enter_context(tc.tile_pool(name="keep", bufs=1))
        raw_pool = stack.enter_context(tc.tile_pool(name="raw_pool", bufs=RAW_BUFS))
        block_pool = stack.enter_context(tc.tile_pool(name="block_pool", bufs=BLOCK_BUFS))
        tail_pool = stack.enter_context(tc.tile_pool(name="tail_pool", bufs=2))
        flip_banks = stack.enter_context(tc.psum_pool(name="flip_banks", bufs=BLOCKS))
        sum_banks = stack.enter_context(tc.psum_pool(name="sum_banks", bufs=BLOCKS))
        stack.enter_context(tc.manual_schedule())

        attn_sb = keep.tile([P, NODE_TILES, CONTEXTS], BF16)
        nc.sync.dma_start(out=attn_sb[:], in_=attn.rearrange("(p t) k -> p t k", t=NODE_TILES))
        BC, BN, BU = slice(0, HIDDEN), slice(HIDDEN, 2 * HIDDEN), slice(2 * HIDDEN, 2 * HIDDEN + OUTPUTS)
        bias_rows = keep.tile([P, 2 * HIDDEN + OUTPUTS], BF16)
        nc.vector.memset(bias_rows[:], 0.0)
        nc.sync.dma_start(out=bias_rows[0:1, BC], in_=bc.unsqueeze(0))
        nc.sync.dma_start(out=bias_rows[0:1, BN], in_=bn.unsqueeze(0))
        nc.sync.dma_start(out=bias_rows[0:1, BU], in_=bu.unsqueeze(0))

        x_blocks = x.rearrange("(p t) f -> p t f", t=NODE_TILES)
        context_blocks = contexts.rearrange("(p t) k f -> p (t k) f", t=NODE_TILES)
        sources = (
            [Wn.rearrange("(b p) f -> p b f", p=P)]
            + [x_blocks[:, b : b + BLOCKS, :] for b in range(0, NODE_TILES, BLOCKS)]
            + [Wc.rearrange("(b p) f -> p b f", p=P)]
            + [context_blocks[:, b : b + BLOCKS, :] for b in range(0, NODE_TILES * CONTEXTS, BLOCKS)]
        )
        out_tiles = out.rearrange("(p t) o -> t p o", t=NODE_TILES)

        rows_of = {}

        def load_round(q):
            raw = raw_pool.tile([P, BLOCKS, FEATURES], BF16)
            nc.sync.dma_start(out=raw[:], in_=sources[q])
            rows_of[q] = raw

        for q in range(CONTEXT_ROUND):
            load_round(q)
        wu_raw = keep.tile([P, OUTPUTS // P, HIDDEN], BF16)
        nc.sync.dma_start(out=wu_raw[:], in_=Wu.rearrange("(b p) h -> p b h", p=P))
        for q in range(CONTEXT_ROUND, RAW_BUFS):
            load_round(q)

        identity_f32 = keep.tile([P, P], F32)
        make_identity(nc, identity_f32[:])
        identity_bf16 = keep.tile([P, P], BF16)
        make_identity(nc, identity_bf16[:])
        ones = keep.tile([P, P], BF16)
        nc.vector.memset(ones[:], 1.0)

        bias_all = keep.tile([P, 2 * HIDDEN + OUTPUTS], F32)
        for cols, width in ((BC, HIDDEN), (BN, HIDDEN), (BU, OUTPUTS)):
            spread = sum_banks.tile([P, width], F32, tag="sums")
            nc.tensor.matmul(out=spread[:], lhsT=ones[:], rhs=bias_rows[:, cols], start=True, stop=True)
            nc.scalar.copy(out=bias_all[:, cols], in_=spread[:])

        weight = keep.tile([P, NODE_TILES, CONTEXTS + 1], F32)
        nc.vector.memset(weight[:], 1.0)
        nc.vector.tensor_scalar_mul(out=weight[:, :, 0:CONTEXTS], in0=attn_sb[:], scalar1=1.0 / CONTEXTS)
        weight_sum = keep.tile([P, NODE_TILES], F32)
        nc.vector.tensor_reduce(
            out=weight_sum[:], in_=weight[:, :, 0:CONTEXTS], axis=mybir.AxisListType.X, op=ALU.add
        )
        running = keep.tile([P, NODE_TILES, HIDDEN], F32)
        for t in range(NODE_TILES):
            nc.vector.scalar_tensor_tensor(
                out=running[:, t, :],
                in0=bias_all[:, BC],
                scalar=weight_sum[:, t : t + 1],
                in1=bias_all[:, BN],
                op0=ALU.mult,
                op1=ALU.add,
            )

        def flip_block(q, j, grouped_words):
            words = rows_of[q][:].bitcast(F32)[:, j, :]
            flipped = flip_banks.tile([P, WORD_PIECES, P], F32, tag="flipped")
            for c in range(WORD_PIECES):
                nc.tensor.transpose(flipped[:, c, :], words[:, c * P : (c + 1) * P], identity_f32[:])
            nc.scalar.copy(out=grouped_words, in_=flipped[:].rearrange("p (g u) r -> p g r u", u=2))
            if j == BLOCKS - 1 and q + RAW_BUFS < ROUNDS:
                load_round(q + RAW_BUFS)

        def flip_round(q):
            grouped_blocks = []
            for j in range(BLOCKS):
                grouped = block_pool.tile([P, PASSES * P * PACK], BF16, align_bytes=64)
                flip_block(
                    q,
                    j,
                    grouped[:].bitcast(F32).rearrange("p (g r u) -> p g r u", g=PASSES, u=2),
                )
                grouped_blocks.append(grouped)
            return grouped_blocks

        def quantise_block(grouped):
            codes = block_pool.tile([P, PASSES * P], U32, align_bytes=64)
            scales = block_pool.tile([P, PASSES * P], U8, align_bytes=64)
            nc.vector.quantize_mx(out=codes[:].bitcast(FP8X4), scales=scales[:], in_=grouped[:])
            return codes, scales

        def flip_weights(q, label):
            grouped = keep.tile([P, PASSES * HIDDEN * PACK], BF16, align_bytes=64, name=label + "_grouped")
            by_block = grouped[:].bitcast(F32).rearrange("p (g b r u) -> p b g r u", g=PASSES, b=BLOCKS, u=2)
            for b in range(BLOCKS):
                flip_block(q, b, by_block[:, b])
            return grouped

        def quantise_weights(grouped, label):
            codes = keep.tile([P, PASSES * HIDDEN], U32, align_bytes=64, name=label + "_codes")
            scales = keep.tile([P, PASSES * HIDDEN], U8, align_bytes=64, name=label + "_scales")
            nc.vector.quantize_mx(out=codes[:].bitcast(FP8X4), scales=scales[:], in_=grouped[:])
            return codes, scales

        def multiply_block(operand, weights):
            codes, scales = operand
            w_codes, w_scales = weights
            sums = sum_banks.tile([P, HIDDEN], F32, tag="sums")
            for g in range(PASSES):
                rows = slice(g * P, (g + 1) * P)
                hidden_cols = slice(g * HIDDEN, (g + 1) * HIDDEN)
                nc.tensor.matmul_mx(
                    out=sums[:],
                    lhsT=codes[:, rows].bitcast(FP8X4),
                    lhsT_scale=scales[:, rows],
                    rhs=w_codes[:, hidden_cols].bitcast(FP8X4),
                    rhs_scale=w_scales[:, hidden_cols],
                    start=(g == 0),
                    stop=(g == PASSES - 1),
                )
            return sums

        def add_weighted(sums, t, column, target):
            nc.vector.scalar_tensor_tensor(
                out=target,
                in0=sums[:],
                scalar=weight[:, t, column : column + 1],
                in1=running[:, t, :],
                op0=ALU.mult,
                op1=ALU.add,
            )

        def flip_hidden(rows, grouped):
            flipped = flip_banks.tile([P, PACK, P], BF16, tag="flipped")
            for c in range(PACK):
                nc.tensor.transpose(flipped[:, c, :], rows[:, c * P : (c + 1) * P], identity_bf16[:])
            nc.scalar.copy(out=grouped, in_=flipped[:].rearrange("p c r -> p r c"))

        def quantise_hidden(grouped, pool, label, count):
            codes = pool.tile([P, count], U32, align_bytes=64, name=label + "_codes")
            scales = pool.tile([P, count], U8, align_bytes=64, name=label + "_scales")
            nc.vector.quantize_mx(
                out=codes[:].bitcast(FP8X4), scales=scales[:], in_=grouped[:].rearrange("p r c -> p (r c)")
            )
            return codes, scales

        def project(operand, weights, t):
            codes, scales = operand
            w_codes, w_scales = weights
            projected = sum_banks.tile([P, OUTPUTS], F32, tag="sums")
            nc.tensor.matmul_mx(
                out=projected[:],
                lhsT=codes[:].bitcast(FP8X4),
                lhsT_scale=scales[:],
                rhs=w_codes[:].bitcast(FP8X4),
                rhs_scale=w_scales[:],
                start=True,
                stop=True,
            )
            result = tail_pool.tile([P, OUTPUTS], F32)
            nc.vector.tensor_tensor(out=result[:], in0=projected[:], in1=bias_all[:, BU], op=ALU.add)
            nc.sync.dma_start(out=out_tiles[t], in_=result[:])

        def tile_finished_in(q):
            contexts_done = (q + 1 - CONTEXT_ROUND) * BLOCKS
            if CONTEXT_ROUND <= q < ROUNDS and contexts_done % CONTEXTS == 0:
                return contexts_done // CONTEXTS - 1
            return None

        weights_of = {}
        hidden_of = {}
        operands = []
        for q in range(-1, ROUNDS + 2):
            coming = q + 1
            coming_is_weights = coming == WN_ROUND or coming == WC_ROUND
            coming_is_rows = coming < ROUNDS and not coming_is_weights

            done = tile_finished_in(q - 2)
            if done is not None:
                hidden_grouped = tail_pool.tile([P, P, PACK], BF16, align_bytes=64)
                flip_hidden(hidden_of[done][:], hidden_grouped[:])
            if coming == WN_ROUND:
                weights_grouped = flip_weights(coming, "wn")
            if coming == WC_ROUND:
                weights_grouped = flip_weights(coming, "wc")
                wu_grouped = keep.tile([P, OUTPUTS, PACK], BF16, align_bytes=64)
                for b in range(OUTPUTS // P):
                    flip_hidden(wu_raw[:, b, :], wu_grouped[:, b * P : (b + 1) * P, :])
            if coming_is_rows:
                grouped_blocks = flip_round(coming)

            if done is not None:
                hidden_operand = quantise_hidden(hidden_grouped, tail_pool, "hidden", P)
            following = []
            for j in range(BLOCKS):
                if coming_is_rows:
                    following.append(quantise_block(grouped_blocks[j]))
                if X_ROUND <= q < WC_ROUND:
                    t = (q - X_ROUND) * BLOCKS + j
                    add_weighted(multiply_block(operands[j], weights_of["wn"]), t, ONE, running[:, t, :])
                if CONTEXT_ROUND <= q < ROUNDS:
                    t, k = divmod((q - CONTEXT_ROUND) * BLOCKS + j, CONTEXTS)
                    sums = multiply_block(operands[j], weights_of["wc"])
                    if k < CONTEXTS - 1:
                        add_weighted(sums, t, k, running[:, t, :])
                    else:
                        hidden = tail_pool.tile([P, HIDDEN], BF16)
                        add_weighted(sums, t, k, hidden[:])
                        hidden_of[t] = hidden
            if coming_is_rows:
                operands = following
            if coming == WN_ROUND:
                weights_of["wn"] = quantise_weights(weights_grouped, "wn")
            if coming == WC_ROUND:
                weights_of["wc"] = quantise_weights(weights_grouped, "wc")
                weights_of["wu"] = quantise_hidden(wu_grouped, keep, "wu", OUTPUTS)
            if done is not None:
                project(hidden_operand, weights_of["wu"], done)
